import numpy as np
import ml_dtypes


def mxq(x, axis, fmt="e4m3"):
    dtype, down = {"e4m3": (ml_dtypes.float8_e4m3fn, 7), "e5m2": (ml_dtypes.float8_e5m2, 14)}[fmt]
    v = np.moveaxis(np.asarray(x, np.float32).astype(ml_dtypes.bfloat16).astype(np.float64), axis, -1)
    blocks = v.reshape(v.shape[:-1] + (-1, 32))
    amax = np.abs(blocks).max(-1, keepdims=True)
    byte = np.maximum(np.where(amax > 0, np.frexp(amax)[1] - 1 + 127, 0) - down, 1)
    scale = np.exp2(byte - 127.0)
    codes = (blocks / scale).astype(np.float32).astype(dtype).astype(np.float64)
    return np.moveaxis((codes * scale).reshape(v.shape), -1, axis)


WIDE = False


def mx_kscale(k):
    if not WIDE:
        return np.ones(k)
    levels = np.array([10, -10, 5, -5, 0])
    a = np.random.permutation(np.resize(levels, k // 512 * 4)).reshape(k // 512, 4)
    idx = np.arange(k)
    return np.exp2(a[idx // 512, idx % 128 // 32])


BF16 = ml_dtypes.bfloat16


def bf(x):
    return np.asarray(x, np.float32).astype(BF16)


def f64(x):
    return np.asarray(x).astype(np.float64)


T, K, D = 8192, 512, 512
ACTIVE = 128.0


def setup_inputs():
    s = mx_kscale(K)
    allow = s <= max(s.min(), s.max() * 2.0 ** -18)
    p = np.maximum(np.random.uniform(-0.15, 1.0, (T, 1)), 0.0) * ACTIVE / K
    on = (np.random.uniform(size=(T, K)) < p) & allow[None, :]
    flags = 0.5 * np.random.uniform(size=(T, K)) + 0.5 * on
    w = np.random.standard_normal((K, D)) * (s / s.min())[:, None]
    return {"flags_matrix": bf(flags), "emb_weight": bf(w)}


def reference(flags_matrix, emb_weight):
    mask = (f64(flags_matrix) > 0.5).astype(np.float64)
    counts = np.sum(mask, axis=1, keepdims=True)
    sums = mxq(mask, 1, "e4m3") @ mxq(f64(emb_weight), 0, "e4m3")
    return np.where(counts > 0, sums / np.maximum(counts, 1.0), 0.0)

@@ -1,0 +1,164 @@
+from contextlib import ExitStack
+
+import concourse.mybir as mybir
+from concourse.masks import make_identity
+
+F32 = mybir.dt.float32
+BF16 = mybir.dt.bfloat16
+U32 = mybir.dt.uint32
+U8 = mybir.dt.uint8
+FP8X4 = mybir.dt.float8_e4m3fn_x4
+ALU = mybir.AluOpType
+ACT = mybir.ActivationFunctionType
+
+P = 128
+T, K, D = 8192, 512, 512
+FLOPS = 2 * T * K * D
+GT = 4
+NG = T // (P * GT)
+CHUNKS = [4, 4, 8, 8, 8, 8, 8, 8, 8]
+MANUAL = False
+CSPLIT = ["vs", "vs", "vv", "vs", "vs", "vs", "vv", "vs", "vs", "vs", "vv", "vs", "vs", "vs", "vv", "vs"]
+
+
+def tile_flagbagencoder_kernel(tc, flags_matrix, emb_weight, out):
+    nc = tc.nc
+    with ExitStack() as ctx:
+        const = ctx.enter_context(tc.tile_pool(name="const", bufs=1))
+        fpool = ctx.enter_context(tc.tile_pool(name="fpool", bufs=1))
+        mpool = ctx.enter_context(tc.tile_pool(name="mpool", bufs=3))
+        gpool = ctx.enter_context(tc.tile_pool(name="gpool", bufs=2))
+        qpool = ctx.enter_context(tc.tile_pool(name="qpool", bufs=3))
+        opool = ctx.enter_context(tc.tile_pool(name="opool", bufs=10))
+        xpsum = ctx.enter_context(tc.psum_pool(name="xpsum", bufs=4))
+        apsum = ctx.enter_context(tc.psum_pool(name="apsum", bufs=4))
+        if MANUAL:
+            ctx.enter_context(tc.manual_schedule())
+
+        wraw = const.tile([P, 4 * D], BF16)
+        nc.scalar.dma_start(
+            out=wraw[:].rearrange("p (u x) -> p u x", u=2),
+            in_=emb_weight.rearrange("(u q e) c -> q u (e c)", u=2, e=2),
+        )
+        groups = []
+        tok0 = 0
+        for ci, nt in enumerate(CHUNKS):
+            ft = fpool.tile([P, nt * K], BF16, name="flags%d" % ci)
+            rows = slice(tok0, tok0 + P * nt)
+            nc.sync.dma_start(out=ft[:], in_=flags_matrix[rows, :].rearrange("(p j) k -> p (j k)", j=nt))
+            oview = out[rows, :].rearrange("(p j) d -> p j d", j=nt)
+            for j0 in range(0, nt, GT):
+                groups.append((ft, j0, oview[:, j0 : j0 + GT, :]))
+            tok0 += P * nt
+        assert len(groups) == NG
+
+        ident = const.tile([P, P], F32)
+        make_identity(nc, ident[:])
+        cnt = const.tile([P, T // P], F32)
+        rc = const.tile([P, T // P], F32)
+        wgrp = const.tile([P, 4 * D], BF16, align_bytes=64)
+        wcodes = const.tile([P, D], U32, align_bytes=64)
+        wscl = const.tile([P, D], U8, align_bytes=64)
+
+        mtiles = {}
+        xts = {}
+        grps = {}
+        quants = {}
+        accs = {}
+
+        def stage_a(g):
+            ft, j0 = groups[g][0], groups[g][1]
+            m = mpool.tile([P, GT * K], BF16, name="mask")
+            for a in range(GT):
+                nc.vector.tensor_scalar(
+                    out=m[:, a * K : (a + 1) * K],
+                    in0=ft[:, (j0 + a) * K : (j0 + a + 1) * K],
+                    scalar1=0.5,
+                    scalar2=None,
+                    op0=ALU.is_gt,
+                    op1=ALU.add,
+                    accum_out=cnt[:, g * GT + a : g * GT + a + 1],
+                )
+            mtiles[g] = m
+
+        def stage_b(g):
+            mw = mtiles[g][:].bitcast(F32)
+            banks = []
+            for b in range(GT // 2):
+                xt = xpsum.tile([P, 4, P], F32, name="xt")
+                for s in range(4):
+                    col = (b * 4 + s) * P
+                    nc.tensor.transpose(xt[:, s, :], mw[:, col : col + P], ident[:])
+                banks.append(xt)
+            xts[g] = banks
+
+        def stage_c(g):
+            gr = gpool.tile([P, GT * K], BF16, name="grouped", align_bytes=64)
+            gw = gr[:].bitcast(F32)
+            for b in range(GT // 2):
+                dst = gw[:, b * 512 : (b + 1) * 512].rearrange("p (a r u) -> p a r u", a=2, u=2)
+                src = xts[g][b][:].rearrange("p (a u) r -> p a r u", u=2)
+                if CSPLIT[g][b] == "v":
+                    nc.vector.tensor_copy(out=dst, in_=src)
+                else:
+                    nc.scalar.copy(out=dst, in_=src)
+            grps[g] = gr
+
+        def stage_d(g):
+            codes = qpool.tile([P, GT * P], U32, name="codes", align_bytes=64)
+            scl = qpool.tile([P, GT * P], U8, name="scl", align_bytes=64)
+            nc.vector.quantize_mx(out=codes[:].bitcast(FP8X4), scales=scl[:], in_=grps[g][:])
+            cols = slice(g * GT, (g + 1) * GT)
+            nc.vector.tensor_scalar_max(rc[:, cols], cnt[:, cols], 1.0)
+            nc.vector.reciprocal(rc[:, cols], rc[:, cols])
+            quants[g] = (codes, scl)
+
+        def stage_e(g):
+            codes, scl = quants[g]
+            lst = []
+            for a in range(GT):
+                acc = apsum.tile([P, D], F32, name="acc")
+                nc.tensor.matmul_mx(
+                    out=acc[:],
+                    lhsT=codes[:, a * P : (a + 1) * P].bitcast(FP8X4),
+                    lhsT_scale=scl[:, a * P : (a + 1) * P],
+                    rhs=wcodes[:].bitcast(FP8X4),
+                    rhs_scale=wscl[:],
+                    start=True,
+                    stop=True,
+                )
+                lst.append(acc)
+            accs[g] = lst
+
+        def stage_f(g):
+            osb = opool.tile([P, GT, D], F32, name="osb")
+            for a in range(GT):
+                nc.scalar.activation(
+                    out=osb[:, a, :],
+                    in_=accs[g][a][:],
+                    func=ACT.Copy,
+                    scale=rc[:, g * GT + a : g * GT + a + 1],
+                )
+            nc.sync.dma_start(out=groups[g][2], in_=osb[:])
+
+        nc.scalar.copy(
+            out=wgrp[:].rearrange("p (c t) -> p c t", t=4),
+            in_=wraw[:].rearrange("p (t c) -> p c t", t=4),
+        )
+        stage_a(0)
+        stage_b(0)
+        stage_a(1)
+        nc.vector.quantize_mx(out=wcodes[:].bitcast(FP8X4), scales=wscl[:], in_=wgrp[:])
+        for i in range(NG + 1):
+            if i >= 1:
+                stage_e(i - 1)
+            if i + 1 < NG:
+                stage_b(i + 1)
+            if i < NG:
+                stage_c(i)
+            if i + 2 < NG:
+                stage_a(i + 2)
+            if i < NG:
+                stage_d(i)
+            if i >= 1:
+                stage_f(i - 1)

@@ -14,11 +14,29 @@ ACT = mybir.ActivationFunctionType
 P = 128
 T, K, D = 8192, 512, 512
 FLOPS = 2 * T * K * D
-GT = 4
-NG = T // (P * GT)
-CHUNKS = [4, 4, 8, 8, 8, 8, 8, 8, 8]
-MANUAL = False
-CSPLIT = ["vs", "vs", "vv", "vs", "vs", "vs", "vv", "vs", "vs", "vs", "vv", "vs", "vs", "vs", "vv", "vs"]
+NT = T // P
+CHUNKS = [2, 2, 4, 8, 16, 32]
+GROUPS = [2, 2] + [4] * 14 + [2, 2]
+NG = len(GROUPS)
+MANUAL = True
+HEAD_S = 4
+VV_PERIOD = 4
+TAIL_V = 3
+W_SPLIT = 256
+
+
+def c_engine(g, b):
+    if g < HEAD_S:
+        return "s"
+    if b == 0 or g % VV_PERIOD == 2:
+        return "v"
+    return "s"
+
+
+def f_engine(g, a):
+    if g >= NG - TAIL_V and a % 2 == 1:
+        return "v"
+    return "s"
 
 
 def tile_flagbagencoder_kernel(tc, flags_matrix, emb_weight, out):
@@ -29,33 +47,34 @@ def tile_flagbagencoder_kernel(tc, flags_matrix, emb_weight, out):
         mpool = ctx.enter_context(tc.tile_pool(name="mpool", bufs=3))
         gpool = ctx.enter_context(tc.tile_pool(name="gpool", bufs=2))
         qpool = ctx.enter_context(tc.tile_pool(name="qpool", bufs=3))
-        opool = ctx.enter_context(tc.tile_pool(name="opool", bufs=10))
+        opool = ctx.enter_context(tc.tile_pool(name="opool", bufs=8))
         xpsum = ctx.enter_context(tc.psum_pool(name="xpsum", bufs=4))
         apsum = ctx.enter_context(tc.psum_pool(name="apsum", bufs=4))
         if MANUAL:
             ctx.enter_context(tc.manual_schedule())
 
         wraw = const.tile([P, 4 * D], BF16)
-        nc.scalar.dma_start(
-            out=wraw[:].rearrange("p (u x) -> p u x", u=2),
-            in_=emb_weight.rearrange("(u q e) c -> q u (e c)", u=2, e=2),
-        )
-        groups = []
+        where = []
         tok0 = 0
         for ci, nt in enumerate(CHUNKS):
             ft = fpool.tile([P, nt * K], BF16, name="flags%d" % ci)
             rows = slice(tok0, tok0 + P * nt)
             nc.sync.dma_start(out=ft[:], in_=flags_matrix[rows, :].rearrange("(p j) k -> p (j k)", j=nt))
+            if ci == 0:
+                nc.sync.dma_start(
+                    out=wraw[:].rearrange("p (u x) -> p u x", u=2),
+                    in_=emb_weight.rearrange("(u q e) c -> q u (e c)", u=2, e=2),
+                )
             oview = out[rows, :].rearrange("(p j) d -> p j d", j=nt)
-            for j0 in range(0, nt, GT):
-                groups.append((ft, j0, oview[:, j0 : j0 + GT, :]))
+            for j in range(nt):
+                where.append((ft, j, oview))
             tok0 += P * nt
-        assert len(groups) == NG
+        first = [sum(GROUPS[:g]) for g in range(NG)]
 
         ident = const.tile([P, P], F32)
         make_identity(nc, ident[:])
-        cnt = const.tile([P, T // P], F32)
-        rc = const.tile([P, T // P], F32)
+        cnt = const.tile([P, NT], F32)
+        rc = const.tile([P, NT], F32)
         wgrp = const.tile([P, 4 * D], BF16, align_bytes=64)
         wcodes = const.tile([P, D], U32, align_bytes=64)
         wscl = const.tile([P, D], U8, align_bytes=64)
@@ -66,25 +85,36 @@ def tile_flagbagencoder_kernel(tc, flags_matrix, emb_weight, out):
         quants = {}
         accs = {}
 
+        def r_max(g):
+            cols = slice(first[g], first[g] + GROUPS[g])
+            nc.vector.tensor_scalar_max(rc[:, cols], cnt[:, cols], 1.0)
+
+        def r_rec(g):
+            cols = slice(first[g], first[g] + GROUPS[g])
+            nc.vector.reciprocal(rc[:, cols], rc[:, cols])
+
         def stage_a(g):
-            ft, j0 = groups[g][0], groups[g][1]
-            m = mpool.tile([P, GT * K], BF16, name="mask")
-            for a in range(GT):
+            n = GROUPS[g]
+            m = mpool.tile([P, n * K], BF16, name="mask")
+            for a in range(n):
+                if a == n // 2 and g >= 1:
+                    r_rec(g - 1)
+                ft, j = where[first[g] + a][0], where[first[g] + a][1]
                 nc.vector.tensor_scalar(
                     out=m[:, a * K : (a + 1) * K],
-                    in0=ft[:, (j0 + a) * K : (j0 + a + 1) * K],
+                    in0=ft[:, j * K : (j + 1) * K],
                     scalar1=0.5,
                     scalar2=None,
                     op0=ALU.is_gt,
                     op1=ALU.add,
-                    accum_out=cnt[:, g * GT + a : g * GT + a + 1],
+                    accum_out=cnt[:, first[g] + a : first[g] + a + 1],
                 )
             mtiles[g] = m
 
         def stage_b(g):
             mw = mtiles[g][:].bitcast(F32)
             banks = []
-            for b in range(GT // 2):
+            for b in range(GROUPS[g] // 2):
                 xt = xpsum.tile([P, 4, P], F32, name="xt")
                 for s in range(4):
                     col = (b * 4 + s) * P
@@ -93,30 +123,27 @@ def tile_flagbagencoder_kernel(tc, flags_matrix, emb_weight, out):
             xts[g] = banks
 
         def stage_c(g):
-            gr = gpool.tile([P, GT * K], BF16, name="grouped", align_bytes=64)
+            gr = gpool.tile([P, GROUPS[g] * K], BF16, name="grouped", align_bytes=64)
             gw = gr[:].bitcast(F32)
-            for b in range(GT // 2):
+            for b in range(GROUPS[g] // 2):
                 dst = gw[:, b * 512 : (b + 1) * 512].rearrange("p (a r u) -> p a r u", a=2, u=2)
                 src = xts[g][b][:].rearrange("p (a u) r -> p a r u", u=2)
-                if CSPLIT[g][b] == "v":
+                if c_engine(g, b) == "v":
                     nc.vector.tensor_copy(out=dst, in_=src)
                 else:
                     nc.scalar.copy(out=dst, in_=src)
             grps[g] = gr
 
         def stage_d(g):
-            codes = qpool.tile([P, GT * P], U32, name="codes", align_bytes=64)
-            scl = qpool.tile([P, GT * P], U8, name="scl", align_bytes=64)
+            codes = qpool.tile([P, GROUPS[g] * P], U32, name="codes", align_bytes=64)
+            scl = qpool.tile([P, GROUPS[g] * P], U8, name="scl", align_bytes=64)
             nc.vector.quantize_mx(out=codes[:].bitcast(FP8X4), scales=scl[:], in_=grps[g][:])
-            cols = slice(g * GT, (g + 1) * GT)
-            nc.vector.tensor_scalar_max(rc[:, cols], cnt[:, cols], 1.0)
-            nc.vector.reciprocal(rc[:, cols], rc[:, cols])
             quants[g] = (codes, scl)
 
         def stage_e(g):
             codes, scl = quants[g]
             lst = []
-            for a in range(GT):
+            for a in range(GROUPS[g]):
                 acc = apsum.tile([P, D], F32, name="acc")
                 nc.tensor.matmul_mx(
                     out=acc[:],
@@ -131,34 +158,49 @@ def tile_flagbagencoder_kernel(tc, flags_matrix, emb_weight, out):
             accs[g] = lst
 
         def stage_f(g):
-            osb = opool.tile([P, GT, D], F32, name="osb")
-            for a in range(GT):
-                nc.scalar.activation(
-                    out=osb[:, a, :],
-                    in_=accs[g][a][:],
-                    func=ACT.Copy,
-                    scale=rc[:, g * GT + a : g * GT + a + 1],
-                )
-            nc.sync.dma_start(out=groups[g][2], in_=osb[:])
+            n = GROUPS[g]
+            osb = opool.tile([P, n, D], F32, name="osb")
+            j0, oview = where[first[g]][1], where[first[g]][2]
+            for a in range(n):
+                t = first[g] + a
+                if f_engine(g, a) == "v":
+                    nc.vector.tensor_scalar(
+                        out=osb[:, a, :], in0=accs[g][a][:], scalar1=rc[:, t : t + 1], scalar2=None, op0=ALU.mult
+                    )
+                else:
+                    nc.scalar.activation(out=osb[:, a, :], in_=accs[g][a][:], func=ACT.Copy, scale=rc[:, t : t + 1])
+                if g == NG - 1:
+                    nc.sync.dma_start(out=oview[:, j0 + a : j0 + a + 1, :], in_=osb[:, a : a + 1, :])
+            if g < NG - 1:
+                nc.sync.dma_start(out=oview[:, j0 : j0 + n, :], in_=osb[:])
 
-        nc.scalar.copy(
-            out=wgrp[:].rearrange("p (c t) -> p c t", t=4),
-            in_=wraw[:].rearrange("p (t c) -> p c t", t=4),
-        )
+        wg3 = wgrp[:].rearrange("p (c t) -> p c t", t=4)
+        wr3 = wraw[:].rearrange("p (t c) -> p c t", t=4)
         stage_a(0)
         stage_b(0)
+        nc.scalar.copy(out=wg3[:, :W_SPLIT, :], in_=wr3[:, :W_SPLIT, :])
+        nc.vector.tensor_copy(out=wg3[:, W_SPLIT:, :], in_=wr3[:, W_SPLIT:, :])
+        r_max(0)
         stage_a(1)
+        stage_b(1)
         nc.vector.quantize_mx(out=wcodes[:].bitcast(FP8X4), scales=wscl[:], in_=wgrp[:])
+        r_max(1)
         for i in range(NG + 1):
             if i >= 1:
                 stage_e(i - 1)
-            if i + 1 < NG:
+            if 1 <= i and i + 1 < NG:
                 stage_b(i + 1)
             if i < NG:
                 stage_c(i)
+            if i < 2:
+                stage_d(i)
             if i + 2 < NG:
                 stage_a(i + 2)
-            if i < NG:
+            elif i + 1 < NG:
+                r_rec(i + 1)
+            if 2 <= i < NG:
                 stage_d(i)
+            if i + 2 < NG:
+                r_max(i + 2)
             if i >= 1:
                 stage_f(i - 1)

@@ -20,21 +20,23 @@ GROUPS = [2, 2] + [4] * 14 + [2, 2]
 NG = len(GROUPS)
 MANUAL = True
 HEAD_S = 4
-VV_PERIOD = 4
-TAIL_V = 3
+F_PERIOD = 4
+TAIL_V = 4
 W_SPLIT = 256
 
 
 def c_engine(g, b):
     if g < HEAD_S:
         return "s"
-    if b == 0 or g % VV_PERIOD == 2:
+    if b == 0:
         return "v"
     return "s"
 
 
 def f_engine(g, a):
-    if g >= NG - TAIL_V and a % 2 == 1:
+    if g >= NG - TAIL_V:
+        return "v" if a % 2 == 1 else "s"
+    if g >= HEAD_S and g % F_PERIOD == 0 and a == 3:
         return "v"
     return "s"
 
@@ -85,20 +87,20 @@ def tile_flagbagencoder_kernel(tc, flags_matrix, emb_weight, out):
         quants = {}
         accs = {}
 
-        def r_max(g):
-            cols = slice(first[g], first[g] + GROUPS[g])
+        def r_max(m):
+            cols = slice(first[2 * m], first[2 * m + 1] + GROUPS[2 * m + 1])
             nc.vector.tensor_scalar_max(rc[:, cols], cnt[:, cols], 1.0)
 
-        def r_rec(g):
-            cols = slice(first[g], first[g] + GROUPS[g])
+        def r_rec(m):
+            cols = slice(first[2 * m], first[2 * m + 1] + GROUPS[2 * m + 1])
             nc.vector.reciprocal(rc[:, cols], rc[:, cols])
 
         def stage_a(g):
             n = GROUPS[g]
             m = mpool.tile([P, n * K], BF16, name="mask")
             for a in range(n):
-                if a == n // 2 and g >= 1:
-                    r_rec(g - 1)
+                if a == n // 2 and g >= 2 and g % 2 == 0:
+                    r_rec(g // 2 - 1)
                 ft, j = where[first[g] + a][0], where[first[g] + a][1]
                 nc.vector.tensor_scalar(
                     out=m[:, a * K : (a + 1) * K],
@@ -180,27 +182,25 @@ def tile_flagbagencoder_kernel(tc, flags_matrix, emb_weight, out):
         stage_b(0)
         nc.scalar.copy(out=wg3[:, :W_SPLIT, :], in_=wr3[:, :W_SPLIT, :])
         nc.vector.tensor_copy(out=wg3[:, W_SPLIT:, :], in_=wr3[:, W_SPLIT:, :])
-        r_max(0)
         stage_a(1)
         stage_b(1)
         nc.vector.quantize_mx(out=wcodes[:].bitcast(FP8X4), scales=wscl[:], in_=wgrp[:])
-        r_max(1)
+        r_max(0)
         for i in range(NG + 1):
-            if i >= 1:
-                stage_e(i - 1)
-            if 1 <= i and i + 1 < NG:
-                stage_b(i + 1)
             if i < NG:
                 stage_c(i)
             if i < 2:
                 stage_d(i)
+                stage_e(i)
             if i + 2 < NG:
                 stage_a(i + 2)
-            elif i + 1 < NG:
-                r_rec(i + 1)
+                stage_b(i + 2)
+            elif i + 2 == NG:
+                r_rec(NG // 2 - 1)
             if 2 <= i < NG:
                 stage_d(i)
-            if i + 2 < NG:
-                r_max(i + 2)
+                stage_e(i)
+            if i % 2 == 1 and i + 2 < NG:
+                r_max((i + 1) // 2)
             if i >= 1:
                 stage_f(i - 1)

@@ -15,20 +15,22 @@ P = 128
 T, K, D = 8192, 512, 512
 FLOPS = 2 * T * K * D
 NT = T // P
-CHUNKS = [2, 2, 4, 8, 16, 32]
+CHUNKS = [2, 2, 4, 8, 8, 8, 32]
+STORES = [2, 2, 4, 8, 8, 8] + [4] * 8
 GROUPS = [2, 2] + [4] * 14 + [2, 2]
 NG = len(GROUPS)
-MANUAL = True
+TINY = 2.0 ** -100
 HEAD_S = 4
 F_PERIOD = 4
-TAIL_V = 4
+TAIL_C = 3
+TAIL_V = 3
 W_SPLIT = 256
 
 
 def c_engine(g, b):
     if g < HEAD_S:
         return "s"
-    if b == 0:
+    if b == 0 or g >= NG - TAIL_C:
         return "v"
     return "s"
 
@@ -49,11 +51,10 @@ def tile_flagbagencoder_kernel(tc, flags_matrix, emb_weight, out):
         mpool = ctx.enter_context(tc.tile_pool(name="mpool", bufs=3))
         gpool = ctx.enter_context(tc.tile_pool(name="gpool", bufs=2))
         qpool = ctx.enter_context(tc.tile_pool(name="qpool", bufs=3))
-        opool = ctx.enter_context(tc.tile_pool(name="opool", bufs=8))
+        opool = ctx.enter_context(tc.tile_pool(name="opool", bufs=6))
         xpsum = ctx.enter_context(tc.psum_pool(name="xpsum", bufs=4))
         apsum = ctx.enter_context(tc.psum_pool(name="apsum", bufs=4))
-        if MANUAL:
-            ctx.enter_context(tc.manual_schedule())
+        ctx.enter_context(tc.manual_schedule())
 
         wraw = const.tile([P, 4 * D], BF16)
         where = []
@@ -72,6 +73,11 @@ def tile_flagbagencoder_kernel(tc, flags_matrix, emb_weight, out):
                 where.append((ft, j, oview))
             tok0 += P * nt
         first = [sum(GROUPS[:g]) for g in range(NG)]
+        results = []
+        osbs = {}
+        for si, ns in enumerate(STORES):
+            for j in range(ns):
+                results.append((si, j, ns))
 
         ident = const.tile([P, P], F32)
         make_identity(nc, ident[:])
@@ -87,13 +93,9 @@ def tile_flagbagencoder_kernel(tc, flags_matrix, emb_weight, out):
         quants = {}
         accs = {}
 
-        def r_max(m):
-            cols = slice(first[2 * m], first[2 * m + 1] + GROUPS[2 * m + 1])
-            nc.vector.tensor_scalar_max(rc[:, cols], cnt[:, cols], 1.0)
-
         def r_rec(m):
             cols = slice(first[2 * m], first[2 * m + 1] + GROUPS[2 * m + 1])
-            nc.vector.reciprocal(rc[:, cols], rc[:, cols])
+            nc.vector.reciprocal(rc[:, cols], cnt[:, cols])
 
         def stage_a(g):
             n = GROUPS[g]
@@ -106,7 +108,7 @@ def tile_flagbagencoder_kernel(tc, flags_matrix, emb_weight, out):
                     out=m[:, a * K : (a + 1) * K],
                     in0=ft[:, j * K : (j + 1) * K],
                     scalar1=0.5,
-                    scalar2=None,
+                    scalar2=TINY,
                     op0=ALU.is_gt,
                     op1=ALU.add,
                     accum_out=cnt[:, first[g] + a : first[g] + a + 1],
@@ -161,20 +163,21 @@ def tile_flagbagencoder_kernel(tc, flags_matrix, emb_weight, out):
 
         def stage_f(g):
             n = GROUPS[g]
-            osb = opool.tile([P, n, D], F32, name="osb")
-            j0, oview = where[first[g]][1], where[first[g]][2]
             for a in range(n):
                 t = first[g] + a
+                si, j, ns = results[t]
+                if j == 0:
+                    osb = opool.tile([P, ns, D], F32, name="osb")
+                    osbs[si] = osb
                 if f_engine(g, a) == "v":
                     nc.vector.tensor_scalar(
-                        out=osb[:, a, :], in0=accs[g][a][:], scalar1=rc[:, t : t + 1], scalar2=None, op0=ALU.mult
+                        out=osbs[si][:, j, :], in0=accs[g][a][:], scalar1=rc[:, t : t + 1], scalar2=None, op0=ALU.mult
                     )
                 else:
-                    nc.scalar.activation(out=osb[:, a, :], in_=accs[g][a][:], func=ACT.Copy, scale=rc[:, t : t + 1])
-                if g == NG - 1:
-                    nc.sync.dma_start(out=oview[:, j0 + a : j0 + a + 1, :], in_=osb[:, a : a + 1, :])
-            if g < NG - 1:
-                nc.sync.dma_start(out=oview[:, j0 : j0 + n, :], in_=osb[:])
+                    nc.scalar.activation(out=osbs[si][:, j, :], in_=accs[g][a][:], func=ACT.Copy, scale=rc[:, t : t + 1])
+                if j == ns - 1:
+                    j0, oview = where[t][1] + 1 - ns, where[t][2]
+                    nc.sync.dma_start(out=oview[:, j0 : j0 + ns, :], in_=osbs[si][:])
 
         wg3 = wgrp[:].rearrange("p (c t) -> p c t", t=4)
         wr3 = wraw[:].rearrange("p (t c) -> p c t", t=4)
@@ -185,7 +188,6 @@ def tile_flagbagencoder_kernel(tc, flags_matrix, emb_weight, out):
         stage_a(1)
         stage_b(1)
         nc.vector.quantize_mx(out=wcodes[:].bitcast(FP8X4), scales=wscl[:], in_=wgrp[:])
-        r_max(0)
         for i in range(NG + 1):
             if i < NG:
                 stage_c(i)
@@ -200,7 +202,5 @@ def tile_flagbagencoder_kernel(tc, flags_matrix, emb_weight, out):
             if 2 <= i < NG:
                 stage_d(i)
                 stage_e(i)
-            if i % 2 == 1 and i + 2 < NG:
-                r_max((i + 1) // 2)
             if i >= 1:
                 stage_f(i - 1)

@@ -16,7 +16,7 @@ T, K, D = 8192, 512, 512
 FLOPS = 2 * T * K * D
 NT = T // P
 CHUNKS = [2, 2, 4, 8, 8, 8, 32]
-STORES = [2, 2, 4, 8, 8, 8] + [4] * 8
+STORES = [2, 2, 4, 8, 8, 8] + [4] * 7 + [2, 1, 1]
 GROUPS = [2, 2] + [4] * 14 + [2, 2]
 NG = len(GROUPS)
 TINY = 2.0 ** -100

from contextlib import ExitStack

import concourse.mybir as mybir
from concourse.masks import make_identity

F32 = mybir.dt.float32
BF16 = mybir.dt.bfloat16
U32 = mybir.dt.uint32
U8 = mybir.dt.uint8
FP8X4 = mybir.dt.float8_e4m3fn_x4
ALU = mybir.AluOpType
ACT = mybir.ActivationFunctionType

P = 128
T, K, D = 8192, 512, 512
FLOPS = 2 * T * K * D
NT = T // P
CHUNKS = [2, 2, 4, 8, 8, 8, 32]
STORES = [2, 2, 4, 8, 8, 8] + [4] * 7 + [2, 1, 1]
GROUPS = [2, 2] + [4] * 14 + [2, 2]
NG = len(GROUPS)
TINY = 2.0 ** -100
HEAD_S = 4
F_PERIOD = 4
TAIL_C = 3
TAIL_V = 3
W_SPLIT = 256


def c_engine(g, b):
    if g < HEAD_S:
        return "s"
    if b == 0 or g >= NG - TAIL_C:
        return "v"
    return "s"


def f_engine(g, a):
    if g >= NG - TAIL_V:
        return "v" if a % 2 == 1 else "s"
    if g >= HEAD_S and g % F_PERIOD == 0 and a == 3:
        return "v"
    return "s"


def tile_flagbagencoder_kernel(tc, flags_matrix, emb_weight, out):
    nc = tc.nc
    with ExitStack() as ctx:
        const = ctx.enter_context(tc.tile_pool(name="const", bufs=1))
        fpool = ctx.enter_context(tc.tile_pool(name="fpool", bufs=1))
        mpool = ctx.enter_context(tc.tile_pool(name="mpool", bufs=3))
        gpool = ctx.enter_context(tc.tile_pool(name="gpool", bufs=2))
        qpool = ctx.enter_context(tc.tile_pool(name="qpool", bufs=3))
        opool = ctx.enter_context(tc.tile_pool(name="opool", bufs=6))
        xpsum = ctx.enter_context(tc.psum_pool(name="xpsum", bufs=4))
        apsum = ctx.enter_context(tc.psum_pool(name="apsum", bufs=4))
        ctx.enter_context(tc.manual_schedule())

        wraw = const.tile([P, 4 * D], BF16)
        where = []
        tok0 = 0
        for ci, nt in enumerate(CHUNKS):
            ft = fpool.tile([P, nt * K], BF16, name="flags%d" % ci)
            rows = slice(tok0, tok0 + P * nt)
            nc.sync.dma_start(out=ft[:], in_=flags_matrix[rows, :].rearrange("(p j) k -> p (j k)", j=nt))
            if ci == 0:
                nc.sync.dma_start(
                    out=wraw[:].rearrange("p (u x) -> p u x", u=2),
                    in_=emb_weight.rearrange("(u q e) c -> q u (e c)", u=2, e=2),
                )
            oview = out[rows, :].rearrange("(p j) d -> p j d", j=nt)
            for j in range(nt):
                where.append((ft, j, oview))
            tok0 += P * nt
        first = [sum(GROUPS[:g]) for g in range(NG)]
        results = []
        osbs = {}
        for si, ns in enumerate(STORES):
            for j in range(ns):
                results.append((si, j, ns))

        ident = const.tile([P, P], F32)
        make_identity(nc, ident[:])
        cnt = const.tile([P, NT], F32)
        rc = const.tile([P, NT], F32)
        wgrp = const.tile([P, 4 * D], BF16, align_bytes=64)
        wcodes = const.tile([P, D], U32, align_bytes=64)
        wscl = const.tile([P, D], U8, align_bytes=64)

        mtiles = {}
        xts = {}
        grps = {}
        quants = {}
        accs = {}

        def r_rec(m):
            cols = slice(first[2 * m], first[2 * m + 1] + GROUPS[2 * m + 1])
            nc.vector.reciprocal(rc[:, cols], cnt[:, cols])

        def stage_a(g):
            n = GROUPS[g]
            m = mpool.tile([P, n * K], BF16, name="mask")
            for a in range(n):
                if a == n // 2 and g >= 2 and g % 2 == 0:
                    r_rec(g // 2 - 1)
                ft, j = where[first[g] + a][0], where[first[g] + a][1]
                nc.vector.tensor_scalar(
                    out=m[:, a * K : (a + 1) * K],
                    in0=ft[:, j * K : (j + 1) * K],
                    scalar1=0.5,
                    scalar2=TINY,
                    op0=ALU.is_gt,
                    op1=ALU.add,
                    accum_out=cnt[:, first[g] + a : first[g] + a + 1],
                )
            mtiles[g] = m

        def stage_b(g):
            mw = mtiles[g][:].bitcast(F32)
            banks = []
            for b in range(GROUPS[g] // 2):
                xt = xpsum.tile([P, 4, P], F32, name="xt")
                for s in range(4):
                    col = (b * 4 + s) * P
                    nc.tensor.transpose(xt[:, s, :], mw[:, col : col + P], ident[:])
                banks.append(xt)
            xts[g] = banks

        def stage_c(g):
            gr = gpool.tile([P, GROUPS[g] * K], BF16, name="grouped", align_bytes=64)
            gw = gr[:].bitcast(F32)
            for b in range(GROUPS[g] // 2):
                dst = gw[:, b * 512 : (b + 1) * 512].rearrange("p (a r u) -> p a r u", a=2, u=2)
                src = xts[g][b][:].rearrange("p (a u) r -> p a r u", u=2)
                if c_engine(g, b) == "v":
                    nc.vector.tensor_copy(out=dst, in_=src)
                else:
                    nc.scalar.copy(out=dst, in_=src)
            grps[g] = gr

        def stage_d(g):
            codes = qpool.tile([P, GROUPS[g] * P], U32, name="codes", align_bytes=64)
            scl = qpool.tile([P, GROUPS[g] * P], U8, name="scl", align_bytes=64)
            nc.vector.quantize_mx(out=codes[:].bitcast(FP8X4), scales=scl[:], in_=grps[g][:])
            quants[g] = (codes, scl)

        def stage_e(g):
            codes, scl = quants[g]
            lst = []
            for a in range(GROUPS[g]):
                acc = apsum.tile([P, D], F32, name="acc")
                nc.tensor.matmul_mx(
                    out=acc[:],
                    lhsT=codes[:, a * P : (a + 1) * P].bitcast(FP8X4),
                    lhsT_scale=scl[:, a * P : (a + 1) * P],
                    rhs=wcodes[:].bitcast(FP8X4),
                    rhs_scale=wscl[:],
                    start=True,
                    stop=True,
                )
                lst.append(acc)
            accs[g] = lst

        def stage_f(g):
            n = GROUPS[g]
            for a in range(n):
                t = first[g] + a
                si, j, ns = results[t]
                if j == 0:
                    osb = opool.tile([P, ns, D], F32, name="osb")
                    osbs[si] = osb
                if f_engine(g, a) == "v":
                    nc.vector.tensor_scalar(
                        out=osbs[si][:, j, :], in0=accs[g][a][:], scalar1=rc[:, t : t + 1], scalar2=None, op0=ALU.mult
                    )
                else:
                    nc.scalar.activation(out=osbs[si][:, j, :], in_=accs[g][a][:], func=ACT.Copy, scale=rc[:, t : t + 1])
                if j == ns - 1:
                    j0, oview = where[t][1] + 1 - ns, where[t][2]
                    nc.sync.dma_start(out=oview[:, j0 : j0 + ns, :], in_=osbs[si][:])

        wg3 = wgrp[:].rearrange("p (c t) -> p c t", t=4)
        wr3 = wraw[:].rearrange("p (t c) -> p c t", t=4)
        stage_a(0)
        stage_b(0)
        nc.scalar.copy(out=wg3[:, :W_SPLIT, :], in_=wr3[:, :W_SPLIT, :])
        nc.vector.tensor_copy(out=wg3[:, W_SPLIT:, :], in_=wr3[:, W_SPLIT:, :])
        stage_a(1)
        stage_b(1)
        nc.vector.quantize_mx(out=wcodes[:].bitcast(FP8X4), scales=wscl[:], in_=wgrp[:])
        for i in range(NG + 1):
            if i < NG:
                stage_c(i)
            if i < 2:
                stage_d(i)
                stage_e(i)
            if i + 2 < NG:
                stage_a(i + 2)
                stage_b(i + 2)
            elif i + 2 == NG:
                r_rec(NG // 2 - 1)
            if 2 <= i < NG:
                stage_d(i)
                stage_e(i)
            if i >= 1:
                stage_f(i - 1)
